import numpy as np
import ml_dtypes


def mxq(x, axis, fmt="e4m3"):
    dtype, down = {"e4m3": (ml_dtypes.float8_e4m3fn, 7), "e5m2": (ml_dtypes.float8_e5m2, 14)}[fmt]
    v = np.moveaxis(np.asarray(x, np.float32).astype(ml_dtypes.bfloat16).astype(np.float64), axis, -1)
    blocks = v.reshape(v.shape[:-1] + (-1, 32))
    amax = np.abs(blocks).max(-1, keepdims=True)
    byte = np.maximum(np.where(amax > 0, np.frexp(amax)[1] - 1 + 127, 0) - down, 1)
    scale = np.exp2(byte - 127.0)
    codes = (blocks / scale).astype(np.float32).astype(dtype).astype(np.float64)
    return np.moveaxis((codes * scale).reshape(v.shape), -1, axis)


WIDE = False


def mx_kscale(k):
    if not WIDE:
        return np.ones(k)
    levels = np.array([10, -10, 5, -5, 0])
    a = np.random.permutation(np.resize(levels, k // 512 * 4)).reshape(k // 512, 4)
    idx = np.arange(k)
    return np.exp2(a[idx // 512, idx % 128 // 32])


BF16 = ml_dtypes.bfloat16


def bf(x):
    return np.asarray(x, np.float32).astype(BF16)


def f64(x):
    return np.asarray(x).astype(np.float64)


B, S, D, E = 4, 1024, 256, 2


def make_adj():
    w = np.random.uniform(size=(B, S, S))
    keep = np.random.uniform(size=(B, S, S)) > 0.6
    return bf(w * keep)


def setup_inputs():
    s = mx_kscale(S)
    a = np.log2(s)
    q = np.random.standard_normal((E, B, S, D)) * 1.4
    k = np.random.standard_normal((E, B, S, D)) * 1.4
    v = np.random.standard_normal((E, B, S, D))
    q[..., 0] = 2.0
    k[..., 0] += -a * np.log(2.0) * np.sqrt(D)
    v = v * (s / s.min())[None, None, :, None]
    return {"q": bf(q), "k": bf(k), "v": bf(v), "adj0": make_adj(), "adj1": make_adj()}


def reference(q, k, v, adj0, adj1):
    adj = np.stack([f64(adj0), f64(adj1)])
    scores = f64(q) @ f64(k).transpose(0, 1, 3, 2) / np.sqrt(D)
    scores = scores * (adj + 1e-6) + np.where(adj == 0, -10000.0, 0.0)
    p = np.exp(scores - scores.max(-1, keepdims=True))
    return (mxq(p, 3, "e4m3") @ mxq(f64(v), 2, "e4m3")) / p.sum(-1, keepdims=True)

@@ -1,0 +1,263 @@
+from contextlib import ExitStack
+
+import concourse.mybir as mybir
+from concourse.masks import make_identity
+
+F32 = mybir.dt.float32
+BF16 = mybir.dt.bfloat16
+U32 = mybir.dt.uint32
+U8 = mybir.dt.uint8
+FP8X4 = mybir.dt.float8_e4m3fn_x4
+ALU = mybir.AluOpType
+ACT = mybir.ActivationFunctionType
+AXIS = mybir.AxisListType
+
+E, B, S, D = 2, 4, 1024, 256
+P = 128
+PACK = 4
+K_PASS = P * PACK
+PASSES = S // K_PASS
+Q_TILES = S // P
+K_BLOCKS = S // P
+BANK = 512
+HALVES = S // BANK
+WORDS = D // 2
+SCALE = 1.0 / 16.0
+MASK = -10000.0
+HEADS = E * B
+TILES = HEADS * Q_TILES
+
+FLOPS = 2 * (2 * E * B * S * S * D)
+
+
+def tile_heterogeneousgraphtransformer_pa_t_kernel(tc, q, k, v, adj0, adj1, out):
+    nc = tc.nc
+    with ExitStack() as ctx:
+        consts = ctx.enter_context(tc.tile_pool(name="consts", bufs=1))
+        loads = ctx.enter_context(tc.tile_pool(name="loads", bufs=2))
+        heads = ctx.enter_context(tc.tile_pool(name="heads", bufs=2))
+        work = ctx.enter_context(tc.tile_pool(name="work", bufs=2))
+        small = ctx.enter_context(tc.tile_pool(name="small", bufs=4))
+        psum_sc = ctx.enter_context(tc.psum_pool(name="psum_sc", bufs=2 * HALVES))
+        psum_tr = ctx.enter_context(tc.psum_pool(name="psum_tr", bufs=3))
+        psum_o = ctx.enter_context(tc.psum_pool(name="psum_o", bufs=1))
+        ctx.enter_context(tc.manual_schedule())
+
+        ident_f32 = consts.tile([P, P], F32)
+        make_identity(nc, ident_f32[:])
+        ident_bf = consts.tile([P, P], BF16)
+        make_identity(nc, ident_bf[:])
+
+        live = {}
+
+        def load_head(h):
+            e, b = divmod(h, B)
+            adj = (adj0, adj1)[e]
+            k_sb = loads.tile([P, K_BLOCKS * D], BF16)
+            nc.sync.dma_start(
+                out=k_sb[:].rearrange("p (t d) -> p t d", d=D), in_=k[e, b].rearrange("(t p) d -> p t d", p=P)
+            )
+            q_sb = loads.tile([P, Q_TILES * D], BF16)
+            nc.sync.dma_start(out=q_sb[:], in_=q[e, b].rearrange("(p j) d -> p (j d)", j=Q_TILES))
+            adj_sb = loads.tile([P, Q_TILES, S], BF16)
+            adj_rows = adj[b].rearrange("(p j) c -> p j c", j=Q_TILES)
+            nc.sync.dma_start(out=adj_sb[:, 0:2, :], in_=adj_rows[:, 0:2, :])
+            v_sb = loads.tile([P, K_BLOCKS, D], BF16)
+            nc.sync.dma_start(out=v_sb[:], in_=v[e, b].rearrange("(t p) d -> p t d", p=P))
+            for j0 in range(2, Q_TILES, 2):
+                nc.sync.dma_start(out=adj_sb[:, j0 : j0 + 2, :], in_=adj_rows[:, j0 : j0 + 2, :])
+            live["k_sb", h], live["q_sb", h], live["adj", h], live["v_sb", h] = k_sb, q_sb, adj_sb, v_sb
+            live["k_t", h] = heads.tile([P, S * 2], BF16, name="k_t")
+            live["q_t", h] = heads.tile([P, S * 2], BF16, name="q_t")
+
+        def transpose_rows(h, piece):
+            which, half = "kq"[piece // HALVES], piece % HALVES
+            words = live[which + "_sb", h][:].bitcast(F32)
+            per_bank = BANK // P
+            bank = psum_tr.tile([P, BANK], F32, tag="tr")
+            for i in range(per_bank):
+                blk = half * per_bank + i
+                nc.tensor.transpose(
+                    bank[:, i * P : (i + 1) * P], words[:, blk * WORDS : (blk + 1) * WORDS], ident_f32[:]
+                )
+            live["bank", h] = bank
+
+        def keep_rows(h, piece):
+            which, half = "kq"[piece // HALVES], piece % HALVES
+            words_t = live[which + "_t", h][:].bitcast(F32)
+            nc.scalar.copy(out=words_t[:, half * BANK : (half + 1) * BANK], in_=live["bank", h][:])
+
+        def regroup_v(h, piece):
+            if piece == 0:
+                live["v_grouped", h] = heads.tile([P, PASSES * D * PACK], BF16, align_bytes=64, name="v_grouped")
+            g, cols = piece // 2, slice((piece % 2) * P, (piece % 2 + 1) * P)
+            nc.scalar.copy(
+                out=live["v_grouped", h][:].rearrange("p (g d t) -> p g d t", g=PASSES, t=PACK)[:, g, cols, :],
+                in_=live["v_sb", h][:].rearrange("p (g t) d -> p g d t", t=PACK)[:, g, cols, :],
+            )
+
+        def quantise_v(h):
+            v_codes = heads.tile([P, PASSES * D], U32, align_bytes=64)
+            v_scales = heads.tile([P, PASSES * D], U8, align_bytes=64)
+            nc.vector.quantize_mx(out=v_codes[:].bitcast(FP8X4), scales=v_scales[:], in_=live["v_grouped", h][:])
+            live["v_codes", h], live["v_scales", h] = v_codes, v_scales
+
+        def scores(i, half):
+            h, j = divmod(i, Q_TILES)
+            q_pairs = live["q_t", h][:].rearrange("w (c e) -> w c e", e=2)
+            k_pairs = live["k_t", h][:].rearrange("w (c e) -> w c e", e=2)
+            sc = psum_sc.tile([P, BANK], F32)
+            for par in range(2):
+                nc.tensor.matmul(
+                    out=sc[:],
+                    lhsT=q_pairs[:, j * P : (j + 1) * P, par],
+                    rhs=k_pairs[:, half * BANK : (half + 1) * BANK, par],
+                    start=(par == 0),
+                    stop=(par == 1),
+                )
+            live["sc", i, half] = sc
+
+        def weigh(i, half):
+            h, j = divmod(i, Q_TILES)
+            if half == 0:
+                live["s16", i] = work.tile([P, S], F32, bufs=4, name="s16")
+            cols = slice(half * BANK, (half + 1) * BANK)
+            nc.vector.scalar_tensor_tensor(
+                out=live["s16", i][:, cols],
+                in0=live["adj", h][:, j, cols],
+                scalar=1e-6,
+                in1=live["sc", i, half][:],
+                op0=ALU.add,
+                op1=ALU.mult,
+            )
+
+        def mask_values(i):
+            h, j = divmod(i, Q_TILES)
+            m16 = work.tile([P, S], F32)
+            nc.vector.tensor_scalar(
+                out=m16[:],
+                in0=live["adj", h][:, j, :],
+                scalar1=0.0,
+                scalar2=MASK / SCALE,
+                op0=ALU.is_equal,
+                op1=ALU.mult,
+            )
+            live["m16", i] = m16
+
+        def add_mask(i):
+            s16 = live["s16", i]
+            nc.gpsimd.tensor_tensor(out=s16[:], in0=s16[:], in1=live["m16", i][:], op=ALU.add)
+
+        def row_max(i):
+            top16 = small.tile([P, 1], F32)
+            nc.vector.tensor_reduce(out=top16[:], in_=live["s16", i][:], axis=AXIS.X, op=ALU.max)
+            live["top16", i] = top16
+
+        def negate_max(i):
+            neg_top = small.tile([P, 1], F32)
+            nc.scalar.mul(out=neg_top[:], in_=live["top16", i][:], mul=-SCALE)
+            live["neg_top", i] = neg_top
+
+        def exponent(i):
+            prob = work.tile([P, S], BF16)
+            row_sum = small.tile([P, 1], F32)
+            nc.scalar.activation(
+                out=prob[:],
+                in_=live["s16", i][:],
+                func=ACT.Exp,
+                bias=live["neg_top", i][:],
+                scale=SCALE,
+                accum_out=row_sum[:],
+            )
+            live["prob", i], live["row_sum", i] = prob, row_sum
+
+        def transpose_p(i):
+            prob_t = psum_tr.tile([P, K_BLOCKS, P], BF16, tag="tr")
+            for t in range(K_BLOCKS):
+                nc.tensor.transpose(prob_t[:, t, :], live["prob", i][:, t * P : (t + 1) * P], ident_bf[:])
+            live["prob_t", i] = prob_t
+
+        def regroup_p(i):
+            p_grouped = work.tile([P, S], BF16, align_bytes=64)
+            nc.scalar.copy(
+                out=p_grouped[:].rearrange("p (g r t) -> p g r t", g=PASSES, t=PACK),
+                in_=live["prob_t", i][:].rearrange("p (g t) r -> p g r t", t=PACK),
+            )
+            live["p_grouped", i] = p_grouped
+
+        def quantise_p(i):
+            p_codes = work.tile([P, PASSES * P], U32, align_bytes=64)
+            p_scales = work.tile([P, PASSES * P], U8, align_bytes=64)
+            nc.vector.quantize_mx(out=p_codes[:].bitcast(FP8X4), scales=p_scales[:], in_=live["p_grouped", i][:])
+            live["p_codes", i], live["p_scales", i] = p_codes, p_scales
+
+        def weighted_sum(i):
+            h = i // Q_TILES
+            acc = psum_o.tile([P, D], F32)
+            for g in range(PASSES):
+                nc.tensor.matmul_mx(
+                    out=acc[:],
+                    lhsT=live["p_codes", i][:, g * P : (g + 1) * P].bitcast(FP8X4),
+                    lhsT_scale=live["p_scales", i][:, g * P : (g + 1) * P],
+                    rhs=live["v_codes", h][:, g * D : (g + 1) * D].bitcast(FP8X4),
+                    rhs_scale=live["v_scales", h][:, g * D : (g + 1) * D],
+                    start=(g == 0),
+                    stop=(g == PASSES - 1),
+                )
+            live["acc", i] = acc
+
+        def invert_sum(i):
+            inv_sum = small.tile([P, 1], F32)
+            nc.vector.reciprocal(out=inv_sum[:], in_=live["row_sum", i][:])
+            live["inv_sum", i] = inv_sum
+
+        def normalise(i):
+            h, j = divmod(i, Q_TILES)
+            e, b = divmod(h, B)
+            o_sb = work.tile([P, D], F32, bufs=3)
+            nc.scalar.activation(out=o_sb[:], in_=live["acc", i][:], func=ACT.Copy, scale=live["inv_sum", i][:])
+            nc.sync.dma_start(out=out[e, b].rearrange("(p j) d -> p j d", j=Q_TILES)[:, j, :], in_=o_sb[:])
+
+        def prepare(part, head, rel):
+            if not 0 <= head < HEADS:
+                return
+            if part == "load" and rel == -8:
+                load_head(head)
+            if part == "tensor" and -6 <= rel < -2:
+                transpose_rows(head, rel + 6)
+            if part == "scalar" and -6 <= rel < -2:
+                keep_rows(head, rel + 6)
+            if part == "scalar" and -2 <= rel < 2:
+                regroup_v(head, rel + 2)
+            if part == "vector" and rel == 2:
+                quantise_v(head)
+
+        def prepare_heads(part, r):
+            now = r // Q_TILES
+            prepare(part, now + 1, r - (now + 1) * Q_TILES)
+            prepare(part, now, r - now * Q_TILES)
+
+        def run(stage, i, *more):
+            if 0 <= i < TILES:
+                stage(i, *more)
+
+        for r in range(-8, TILES + 6):
+            prepare_heads("load", r)
+            run(weigh, r, 0)
+            run(scores, r + 2, 0)
+            run(weighted_sum, r - 5)
+            prepare_heads("tensor", r)
+            run(regroup_p, r - 4)
+            run(row_max, r - 2)
+            run(exponent, r - 3)
+            run(weigh, r, 1)
+            run(scores, r + 2, 1)
+            run(transpose_p, r - 3)
+            run(normalise, r - 5)
+            prepare_heads("scalar", r)
+            run(negate_max, r - 2)
+            run(quantise_p, r - 4)
+            run(invert_sum, r - 4)
+            prepare_heads("vector", r)
+            run(mask_values, r)
+            run(add_mask, r)

@@ -15,6 +15,7 @@ AXIS = mybir.AxisListType
 E, B, S, D = 2, 4, 1024, 256
 P = 128
 PACK = 4
+PAIRS = PACK // 2
 K_PASS = P * PACK
 PASSES = S // K_PASS
 Q_TILES = S // P
@@ -45,8 +46,6 @@ def tile_heterogeneousgraphtransformer_pa_t_kernel(tc, q, k, v, adj0, adj1, out)
 
         ident_f32 = consts.tile([P, P], F32)
         make_identity(nc, ident_f32[:])
-        ident_bf = consts.tile([P, P], BF16)
-        make_identity(nc, ident_bf[:])
 
         live = {}
 
@@ -63,7 +62,10 @@ def tile_heterogeneousgraphtransformer_pa_t_kernel(tc, q, k, v, adj0, adj1, out)
             adj_rows = adj[b].rearrange("(p j) c -> p j c", j=Q_TILES)
             nc.sync.dma_start(out=adj_sb[:, 0:2, :], in_=adj_rows[:, 0:2, :])
             v_sb = loads.tile([P, K_BLOCKS, D], BF16)
-            nc.sync.dma_start(out=v_sb[:], in_=v[e, b].rearrange("(t p) d -> p t d", p=P))
+            nc.sync.dma_start(
+                out=v_sb[:].rearrange("p (g t) d -> p g t d", t=PACK),
+                in_=v[e, b].rearrange("(g p t) d -> p g t d", p=P, t=PACK),
+            )
             for j0 in range(2, Q_TILES, 2):
                 nc.sync.dma_start(out=adj_sb[:, j0 : j0 + 2, :], in_=adj_rows[:, j0 : j0 + 2, :])
             live["k_sb", h], live["q_sb", h], live["adj", h], live["v_sb", h] = k_sb, q_sb, adj_sb, v_sb
@@ -172,16 +174,23 @@ def tile_heterogeneousgraphtransformer_pa_t_kernel(tc, q, k, v, adj0, adj1, out)
             live["prob", i], live["row_sum", i] = prob, row_sum
 
         def transpose_p(i):
-            prob_t = psum_tr.tile([P, K_BLOCKS, P], BF16, tag="tr")
-            for t in range(K_BLOCKS):
-                nc.tensor.transpose(prob_t[:, t, :], live["prob", i][:, t * P : (t + 1) * P], ident_bf[:])
+            words = live["prob", i][:].bitcast(F32)
+            prob_t = psum_tr.tile([P, BANK], F32, tag="tr")
+            for g in range(PASSES):
+                for u in range(PAIRS):
+                    blk = PAIRS * g + u
+                    nc.tensor.transpose(
+                        prob_t[:, blk * P : (blk + 1) * P],
+                        words[:, g * PAIRS * P + u : (g + 1) * PAIRS * P : PAIRS],
+                        ident_f32[:],
+                    )
             live["prob_t", i] = prob_t
 
         def regroup_p(i):
             p_grouped = work.tile([P, S], BF16, align_bytes=64)
             nc.scalar.copy(
-                out=p_grouped[:].rearrange("p (g r t) -> p g r t", g=PASSES, t=PACK),
-                in_=live["prob_t", i][:].rearrange("p (g t) r -> p g r t", t=PACK),
+                out=p_grouped[:].bitcast(F32).rearrange("p (g r u) -> p g r u", g=PASSES, u=PAIRS),
+                in_=live["prob_t", i][:].rearrange("p (g u r) -> p g r u", g=PASSES, u=PAIRS),
             )
             live["p_grouped", i] = p_grouped
 

@@ -265,8 +265,8 @@ def tile_heterogeneousgraphtransformer_pa_t_kernel(tc, q, k, v, adj0, adj1, out)
             run(normalise, r - 5)
             prepare_heads("scalar", r)
             run(negate_max, r - 2)
+            run(mask_values, r)
             run(quantise_p, r - 4)
             run(invert_sum, r - 4)
             prepare_heads("vector", r)
-            run(mask_values, r)
             run(add_mask, r)

@@ -26,7 +26,9 @@ WORDS = D // 2
 SCALE = 1.0 / 16.0
 MASK = -10000.0
 HEADS = E * B
-TILES = HEADS * Q_TILES
+DUO = 2
+DUOS = HEADS * Q_TILES // DUO
+HEAD_DUOS = Q_TILES // DUO
 
 FLOPS = 2 * (2 * E * B * S * S * D)
 
@@ -39,7 +41,7 @@ def tile_heterogeneousgraphtransformer_pa_t_kernel(tc, q, k, v, adj0, adj1, out)
         heads = ctx.enter_context(tc.tile_pool(name="heads", bufs=2))
         work = ctx.enter_context(tc.tile_pool(name="work", bufs=2))
         small = ctx.enter_context(tc.tile_pool(name="small", bufs=4))
-        psum_sc = ctx.enter_context(tc.psum_pool(name="psum_sc", bufs=2 * HALVES))
+        psum_sc = ctx.enter_context(tc.psum_pool(name="psum_sc", bufs=DUO * HALVES))
         psum_tr = ctx.enter_context(tc.psum_pool(name="psum_tr", bufs=3))
         psum_o = ctx.enter_context(tc.psum_pool(name="psum_o", bufs=1))
         ctx.enter_context(tc.manual_schedule())
@@ -49,28 +51,32 @@ def tile_heterogeneousgraphtransformer_pa_t_kernel(tc, q, k, v, adj0, adj1, out)
 
         live = {}
 
-        def load_head(h):
+        def load_qk(h):
             e, b = divmod(h, B)
-            adj = (adj0, adj1)[e]
             k_sb = loads.tile([P, K_BLOCKS * D], BF16)
             nc.sync.dma_start(
                 out=k_sb[:].rearrange("p (t d) -> p t d", d=D), in_=k[e, b].rearrange("(t p) d -> p t d", p=P)
             )
             q_sb = loads.tile([P, Q_TILES * D], BF16)
             nc.sync.dma_start(out=q_sb[:], in_=q[e, b].rearrange("(p j) d -> p (j d)", j=Q_TILES))
+            live["k_sb", h], live["q_sb", h] = k_sb, q_sb
+            live["k_t", h] = heads.tile([P, S * 2], BF16, name="k_t")
+            live["q_t", h] = heads.tile([P, S * 2], BF16, name="q_t")
+
+        def load_adj_v(h):
+            e, b = divmod(h, B)
+            adj = (adj0, adj1)[e]
             adj_sb = loads.tile([P, Q_TILES, S], BF16)
             adj_rows = adj[b].rearrange("(p j) c -> p j c", j=Q_TILES)
-            nc.sync.dma_start(out=adj_sb[:, 0:2, :], in_=adj_rows[:, 0:2, :])
+            nc.sync.dma_start(out=adj_sb[:, 0:DUO, :], in_=adj_rows[:, 0:DUO, :])
             v_sb = loads.tile([P, K_BLOCKS, D], BF16)
             nc.sync.dma_start(
                 out=v_sb[:].rearrange("p (g t) d -> p g t d", t=PACK),
                 in_=v[e, b].rearrange("(g p t) d -> p g t d", p=P, t=PACK),
             )
-            for j0 in range(2, Q_TILES, 2):
-                nc.sync.dma_start(out=adj_sb[:, j0 : j0 + 2, :], in_=adj_rows[:, j0 : j0 + 2, :])
-            live["k_sb", h], live["q_sb", h], live["adj", h], live["v_sb", h] = k_sb, q_sb, adj_sb, v_sb
-            live["k_t", h] = heads.tile([P, S * 2], BF16, name="k_t")
-            live["q_t", h] = heads.tile([P, S * 2], BF16, name="q_t")
+            for j0 in range(DUO, Q_TILES, DUO):
+                nc.sync.dma_start(out=adj_sb[:, j0 : j0 + DUO, :], in_=adj_rows[:, j0 : j0 + DUO, :])
+            live["adj", h], live["v_sb", h] = adj_sb, v_sb
 
         def transpose_rows(h, piece):
             which, half = "kq"[piece // HALVES], piece % HALVES
@@ -104,11 +110,15 @@ def tile_heterogeneousgraphtransformer_pa_t_kernel(tc, q, k, v, adj0, adj1, out)
             nc.vector.quantize_mx(out=v_codes[:].bitcast(FP8X4), scales=v_scales[:], in_=live["v_grouped", h][:])
             live["v_codes", h], live["v_scales", h] = v_codes, v_scales
 
-        def scores(i, half):
-            h, j = divmod(i, Q_TILES)
+        def place(r, t):
+            h, d = divmod(r, HEAD_DUOS)
+            return h, d * DUO + t
+
+        def scores(r, t, half):
+            h, j = place(r, t)
             q_pairs = live["q_t", h][:].rearrange("w (c e) -> w c e", e=2)
             k_pairs = live["k_t", h][:].rearrange("w (c e) -> w c e", e=2)
-            sc = psum_sc.tile([P, BANK], F32)
+            sc = psum_sc.tile([P, BANK], F32, tag="sc")
             for par in range(2):
                 nc.tensor.matmul(
                     out=sc[:],
@@ -117,156 +127,230 @@ def tile_heterogeneousgraphtransformer_pa_t_kernel(tc, q, k, v, adj0, adj1, out)
                     start=(par == 0),
                     stop=(par == 1),
                 )
-            live["sc", i, half] = sc
+            live["sc", r, t, half] = sc
 
-        def weigh(i, half):
-            h, j = divmod(i, Q_TILES)
-            if half == 0:
-                live["s16", i] = work.tile([P, S], F32, bufs=4, name="s16")
+        def weigh(r, t, half):
+            h, j = place(r, t)
+            if t == 0 and half == 0:
+                live["s16", r] = work.tile([P, DUO, S], F32, bufs=4, name="s16")
             cols = slice(half * BANK, (half + 1) * BANK)
             nc.vector.scalar_tensor_tensor(
-                out=live["s16", i][:, cols],
+                out=live["s16", r][:, t, cols],
                 in0=live["adj", h][:, j, cols],
                 scalar=1e-6,
-                in1=live["sc", i, half][:],
+                in1=live["sc", r, t, half][:],
                 op0=ALU.add,
                 op1=ALU.mult,
             )
 
-        def mask_values(i):
-            h, j = divmod(i, Q_TILES)
-            m16 = work.tile([P, S], F32)
+        def mask_values(r):
+            h, j = place(r, 0)
+            m16 = work.tile([P, DUO, S], F32)
             nc.vector.tensor_scalar(
                 out=m16[:],
-                in0=live["adj", h][:, j, :],
+                in0=live["adj", h][:, j : j + DUO, :],
                 scalar1=0.0,
                 scalar2=MASK / SCALE,
                 op0=ALU.is_equal,
                 op1=ALU.mult,
             )
-            live["m16", i] = m16
+            live["m16", r] = m16
 
-        def add_mask(i):
-            s16 = live["s16", i]
-            nc.gpsimd.tensor_tensor(out=s16[:], in0=s16[:], in1=live["m16", i][:], op=ALU.add)
+        def add_mask(r, engine, tiles):
+            s16 = live["s16", r][:, tiles, :]
+            engine.tensor_tensor(out=s16, in0=s16, in1=live["m16", r][:, tiles, :], op=ALU.add)
 
-        def row_max(i):
-            top16 = small.tile([P, 1], F32)
-            nc.vector.tensor_reduce(out=top16[:], in_=live["s16", i][:], axis=AXIS.X, op=ALU.max)
-            live["top16", i] = top16
-
-        def negate_max(i):
-            neg_top = small.tile([P, 1], F32)
-            nc.scalar.mul(out=neg_top[:], in_=live["top16", i][:], mul=-SCALE)
-            live["neg_top", i] = neg_top
-
-        def exponent(i):
-            prob = work.tile([P, S], BF16)
-            row_sum = small.tile([P, 1], F32)
-            nc.scalar.activation(
-                out=prob[:],
-                in_=live["s16", i][:],
-                func=ACT.Exp,
-                bias=live["neg_top", i][:],
-                scale=SCALE,
-                accum_out=row_sum[:],
+        def row_max(r, tiles):
+            if tiles.start == 0:
+                live["top16", r] = small.tile([P, DUO], F32, name="top16")
+            nc.vector.tensor_reduce(
+                out=live["top16", r][:, tiles], in_=live["s16", r][:, tiles, :], axis=AXIS.X, op=ALU.max
             )
-            live["prob", i], live["row_sum", i] = prob, row_sum
 
-        def transpose_p(i):
-            words = live["prob", i][:].bitcast(F32)
+        def negate_max(r, tiles):
+            if tiles.start == 0:
+                live["neg_top", r] = small.tile([P, DUO], F32, name="neg_top")
+            nc.scalar.mul(out=live["neg_top", r][:, tiles], in_=live["top16", r][:, tiles], mul=-SCALE)
+
+        def exponent(r, t):
+            if t == 0:
+                live["prob", r] = work.tile([P, DUO, S], BF16, name="prob")
+                live["row_sum", r] = small.tile([P, DUO], F32, name="row_sum")
+            nc.scalar.activation(
+                out=live["prob", r][:, t, :],
+                in_=live["s16", r][:, t, :],
+                func=ACT.Exp,
+                bias=live["neg_top", r][:, t : t + 1],
+                scale=SCALE,
+                accum_out=live["row_sum", r][:, t : t + 1],
+            )
+
+        def transpose_p(r, t):
+            words = live["prob", r][:].rearrange("p t c -> p (t c)").bitcast(F32)
+            first = t * S // 2
             prob_t = psum_tr.tile([P, BANK], F32, tag="tr")
             for g in range(PASSES):
                 for u in range(PAIRS):
                     blk = PAIRS * g + u
                     nc.tensor.transpose(
                         prob_t[:, blk * P : (blk + 1) * P],
-                        words[:, g * PAIRS * P + u : (g + 1) * PAIRS * P : PAIRS],
+                        words[:, first + g * PAIRS * P + u : first + (g + 1) * PAIRS * P : PAIRS],
                         ident_f32[:],
                     )
-            live["prob_t", i] = prob_t
+            live["prob_t", r, t] = prob_t
 
-        def regroup_p(i):
-            p_grouped = work.tile([P, S], BF16, align_bytes=64)
-            nc.scalar.copy(
-                out=p_grouped[:].bitcast(F32).rearrange("p (g r u) -> p g r u", g=PASSES, u=PAIRS),
-                in_=live["prob_t", i][:].rearrange("p (g u r) -> p g r u", g=PASSES, u=PAIRS),
+        def regroup_p(r, t, copy):
+            if t == 0:
+                live["p_grouped", r] = work.tile([P, DUO * S], BF16, align_bytes=64, name="p_grouped")
+            copy(
+                out=live["p_grouped", r][:, t * S : (t + 1) * S]
+                .bitcast(F32)
+                .rearrange("p (g r u) -> p g r u", g=PASSES, u=PAIRS),
+                in_=live["prob_t", r, t][:].rearrange("p (g u r) -> p g r u", g=PASSES, u=PAIRS),
             )
-            live["p_grouped", i] = p_grouped
 
-        def quantise_p(i):
-            p_codes = work.tile([P, PASSES * P], U32, align_bytes=64)
-            p_scales = work.tile([P, PASSES * P], U8, align_bytes=64)
-            nc.vector.quantize_mx(out=p_codes[:].bitcast(FP8X4), scales=p_scales[:], in_=live["p_grouped", i][:])
-            live["p_codes", i], live["p_scales", i] = p_codes, p_scales
+        def quantise_p(r, tiles):
+            if tiles.start == 0:
+                live["p_codes", r] = work.tile([P, DUO * PASSES * P], U32, align_bytes=64, name="p_codes")
+                live["p_scales", r] = work.tile([P, DUO * PASSES * P], U8, align_bytes=64, name="p_scales")
+            words = slice(tiles.start * PASSES * P, tiles.stop * PASSES * P)
+            nc.vector.quantize_mx(
+                out=live["p_codes", r][:, words].bitcast(FP8X4),
+                scales=live["p_scales", r][:, words],
+                in_=live["p_grouped", r][:, tiles.start * S : tiles.stop * S],
+            )
 
-        def weighted_sum(i):
-            h = i // Q_TILES
-            acc = psum_o.tile([P, D], F32)
+        def weighted_sum(r, t, pool, tag):
+            h = r // HEAD_DUOS
+            if t == 0:
+                live["acc", r] = pool.tile([P, DUO * D], F32, tag=tag, name="acc")
             for g in range(PASSES):
+                words = slice((t * PASSES + g) * P, (t * PASSES + g + 1) * P)
                 nc.tensor.matmul_mx(
-                    out=acc[:],
-                    lhsT=live["p_codes", i][:, g * P : (g + 1) * P].bitcast(FP8X4),
-                    lhsT_scale=live["p_scales", i][:, g * P : (g + 1) * P],
+                    out=live["acc", r][:, t * D : (t + 1) * D],
+                    lhsT=live["p_codes", r][:, words].bitcast(FP8X4),
+                    lhsT_scale=live["p_scales", r][:, words],
                     rhs=live["v_codes", h][:, g * D : (g + 1) * D].bitcast(FP8X4),
                     rhs_scale=live["v_scales", h][:, g * D : (g + 1) * D],
                     start=(g == 0),
                     stop=(g == PASSES - 1),
                 )
-            live["acc", i] = acc
 
-        def invert_sum(i):
-            inv_sum = small.tile([P, 1], F32)
-            nc.vector.reciprocal(out=inv_sum[:], in_=live["row_sum", i][:])
-            live["inv_sum", i] = inv_sum
+        def invert_sum(r):
+            inv_sum = small.tile([P, DUO], F32)
+            nc.vector.reciprocal(out=inv_sum[:], in_=live["row_sum", r][:])
+            live["inv_sum", r] = inv_sum
 
-        def normalise(i):
-            h, j = divmod(i, Q_TILES)
+        def normalise(r, t):
+            if t == 0:
+                live["o_sb", r] = work.tile([P, DUO, D], F32, name="o_sb")
+            nc.scalar.activation(
+                out=live["o_sb", r][:, t, :],
+                in_=live["acc", r][:, t * D : (t + 1) * D],
+                func=ACT.Copy,
+                scale=live["inv_sum", r][:, t : t + 1],
+            )
+
+        def store(r, tiles):
+            h, j = place(r, 0)
             e, b = divmod(h, B)
-            o_sb = work.tile([P, D], F32, bufs=3)
-            nc.scalar.activation(out=o_sb[:], in_=live["acc", i][:], func=ACT.Copy, scale=live["inv_sum", i][:])
-            nc.sync.dma_start(out=out[e, b].rearrange("(p j) d -> p j d", j=Q_TILES)[:, j, :], in_=o_sb[:])
+            rows = out[e, b].rearrange("(p j) d -> p j d", j=Q_TILES)
+            nc.sync.dma_start(out=rows[:, j + tiles.start : j + tiles.stop, :], in_=live["o_sb", r][:, tiles, :])
 
         def prepare(part, head, rel):
             if not 0 <= head < HEADS:
                 return
-            if part == "load" and rel == -8:
-                load_head(head)
-            if part == "tensor" and -6 <= rel < -2:
-                transpose_rows(head, rel + 6)
-            if part == "scalar" and -6 <= rel < -2:
-                keep_rows(head, rel + 6)
+            if part == "load" and rel == -6:
+                load_qk(head)
+            if part == "load" and rel == -4:
+                load_adj_v(head)
+            if part == "tensor" and -5 <= rel < -1:
+                transpose_rows(head, rel + 5)
+            if part == "scalar" and -5 <= rel < -1:
+                keep_rows(head, rel + 5)
             if part == "scalar" and -2 <= rel < 2:
                 regroup_v(head, rel + 2)
             if part == "vector" and rel == 2:
                 quantise_v(head)
 
         def prepare_heads(part, r):
-            now = r // Q_TILES
-            prepare(part, now + 1, r - (now + 1) * Q_TILES)
-            prepare(part, now, r - now * Q_TILES)
+            now = r // HEAD_DUOS
+            for head in (now + 2, now + 1, now):
+                prepare(part, head, r - head * HEAD_DUOS)
 
-        def run(stage, i, *more):
-            if 0 <= i < TILES:
-                stage(i, *more)
+        def run(stage, r, *more):
+            if 0 <= r < DUOS:
+                stage(r, *more)
 
-        for r in range(-8, TILES + 6):
+        BOTH, FIRST, SECOND = slice(0, 2), slice(0, 1), slice(1, 2)
+        LAST = DUOS - 1
+
+        for r in range(-6, DUOS):
             prepare_heads("load", r)
-            run(weigh, r, 0)
-            run(scores, r + 2, 0)
-            run(weighted_sum, r - 5)
+            for t in range(DUO):
+                for half in range(HALVES):
+                    run(weigh, r, t, half)
+                    run(scores, r + 1, t, half)
             prepare_heads("tensor", r)
-            run(regroup_p, r - 4)
-            run(row_max, r - 2)
-            run(exponent, r - 3)
-            run(weigh, r, 1)
-            run(scores, r + 2, 1)
-            run(transpose_p, r - 3)
-            run(normalise, r - 5)
+            run(row_max, r - 2, BOTH)
+            run(negate_max, r - 2, BOTH)
+            run(exponent, r - 2, 0)
+            run(exponent, r - 2, 1)
             prepare_heads("scalar", r)
-            run(negate_max, r - 2)
+            run(transpose_p, r - 2, 0)
             run(mask_values, r)
-            run(quantise_p, r - 4)
-            run(invert_sum, r - 4)
+            run(quantise_p, r - 3, BOTH)
+            run(invert_sum, r - 3)
             prepare_heads("vector", r)
-            run(add_mask, r)
+            run(weighted_sum, r - 3, 0, psum_o, "acc")
+            run(weighted_sum, r - 3, 1, psum_o, "acc")
+            run(transpose_p, r - 2, 1)
+            run(normalise, r - 3, 0)
+            run(normalise, r - 3, 1)
+            run(store, r - 3, BOTH)
+            run(regroup_p, r - 2, 0, nc.scalar.copy)
+            run(regroup_p, r - 2, 1, nc.scalar.copy)
+            run(add_mask, r, nc.gpsimd, FIRST if r == LAST else BOTH)
+
+        row_max(LAST - 1, BOTH)
+        row_max(LAST, FIRST)
+        add_mask(LAST, nc.vector, SECOND)
+        row_max(LAST, SECOND)
+        quantise_p(LAST - 2, BOTH)
+        invert_sum(LAST - 2)
+        negate_max(LAST - 1, BOTH)
+        exponent(LAST - 1, 0)
+        transpose_p(LAST - 1, 0)
+        exponent(LAST - 1, 1)
+        transpose_p(LAST - 1, 1)
+        for t in range(DUO):
+            weighted_sum(LAST - 2, t, psum_o, "acc")
+        for t in range(DUO):
+            regroup_p(LAST - 1, t, nc.vector.tensor_copy)
+        quantise_p(LAST - 1, BOTH)
+        invert_sum(LAST - 1)
+        negate_max(LAST, FIRST)
+        exponent(LAST, 0)
+        transpose_p(LAST, 0)
+        negate_max(LAST, SECOND)
+        exponent(LAST, 1)
+        transpose_p(LAST, 1)
+        normalise(LAST - 2, 0)
+        normalise(LAST - 2, 1)
+        store(LAST - 2, BOTH)
+        regroup_p(LAST, 0, nc.vector.tensor_copy)
+        quantise_p(LAST, FIRST)
+        regroup_p(LAST, 1, nc.vector.tensor_copy)
+        quantise_p(LAST, SECOND)
+        invert_sum(LAST)
+        for t in range(DUO):
+            weighted_sum(LAST - 1, t, psum_sc, "sc")
+        normalise(LAST - 1, 0)
+        normalise(LAST - 1, 1)
+        store(LAST - 1, BOTH)
+        for t in range(DUO):
+            weighted_sum(LAST, t, psum_sc, "sc")
+        normalise(LAST, 0)
+        store(LAST, FIRST)
+        normalise(LAST, 1)
+        store(LAST, SECOND)

@@ -24,7 +24,11 @@ BANK = 512
 HALVES = S // BANK
 WORDS = D // 2
 SCALE = 1.0 / 16.0
-MASK = -10000.0
+SHRINK = 2.0**-16
+UNSHRINK = SCALE / SHRINK
+MASKED = 10000.0 / UNSHRINK
+STEEP = 3.0e38
+SCALAR_COLS = 384
 HEADS = E * B
 DUO = 2
 DUOS = HEADS * Q_TILES // DUO
@@ -49,6 +53,11 @@ def tile_heterogeneousgraphtransformer_pa_t_kernel(tc, q, k, v, adj0, adj1, out)
         ident_f32 = consts.tile([P, P], F32)
         make_identity(nc, ident_f32[:])
 
+        ident_bf = consts.tile([P, P], BF16)
+        make_identity(nc, ident_bf[:])
+        masked = consts.tile([P, 1], F32)
+        nc.vector.memset(masked[:], MASKED)
+
         live = {}
 
         def load_qk(h):
@@ -61,7 +70,7 @@ def tile_heterogeneousgraphtransformer_pa_t_kernel(tc, q, k, v, adj0, adj1, out)
             nc.sync.dma_start(out=q_sb[:], in_=q[e, b].rearrange("(p j) d -> p (j d)", j=Q_TILES))
             live["k_sb", h], live["q_sb", h] = k_sb, q_sb
             live["k_t", h] = heads.tile([P, S * 2], BF16, name="k_t")
-            live["q_t", h] = heads.tile([P, S * 2], BF16, name="q_t")
+            live["q_t", h] = heads.tile([P, 2, S], BF16, name="q_t")
 
         def load_adj_v(h):
             e, b = divmod(h, B)
@@ -79,9 +88,21 @@ def tile_heterogeneousgraphtransformer_pa_t_kernel(tc, q, k, v, adj0, adj1, out)
             live["adj", h], live["v_sb", h] = adj_sb, v_sb
 
         def transpose_rows(h, piece):
-            which, half = "kq"[piece // HALVES], piece % HALVES
-            words = live[which + "_sb", h][:].bitcast(F32)
+            half = piece % HALVES
             per_bank = BANK // P
+            if piece >= HALVES:
+                bank = psum_tr.tile([P, 2, BANK], BF16, tag="tr")
+                for i in range(per_bank):
+                    blk = half * per_bank + i
+                    for e in range(2):
+                        nc.tensor.transpose(
+                            bank[:, e, i * P : (i + 1) * P],
+                            live["q_sb", h][:, blk * D + e : (blk + 1) * D : 2],
+                            ident_bf[:],
+                        )
+                live["bank", h] = bank
+                return
+            words = live["k_sb", h][:].bitcast(F32)
             bank = psum_tr.tile([P, BANK], F32, tag="tr")
             for i in range(per_bank):
                 blk = half * per_bank + i
@@ -91,9 +112,14 @@ def tile_heterogeneousgraphtransformer_pa_t_kernel(tc, q, k, v, adj0, adj1, out)
             live["bank", h] = bank
 
         def keep_rows(h, piece):
-            which, half = "kq"[piece // HALVES], piece % HALVES
-            words_t = live[which + "_t", h][:].bitcast(F32)
-            nc.scalar.copy(out=words_t[:, half * BANK : (half + 1) * BANK], in_=live["bank", h][:])
+            half = piece % HALVES
+            cols = slice(half * BANK, (half + 1) * BANK)
+            if piece >= HALVES:
+                nc.scalar.activation(
+                    out=live["q_t", h][:, :, cols], in_=live["bank", h][:], func=ACT.Copy, scale=SHRINK
+                )
+            else:
+                nc.scalar.copy(out=live["k_t", h][:].bitcast(F32)[:, cols], in_=live["bank", h][:])
 
         def regroup_v(h, piece):
             if piece == 0:
@@ -116,13 +142,12 @@ def tile_heterogeneousgraphtransformer_pa_t_kernel(tc, q, k, v, adj0, adj1, out)
 
         def scores(r, t, half):
             h, j = place(r, t)
-            q_pairs = live["q_t", h][:].rearrange("w (c e) -> w c e", e=2)
             k_pairs = live["k_t", h][:].rearrange("w (c e) -> w c e", e=2)
             sc = psum_sc.tile([P, BANK], F32, tag="sc")
             for par in range(2):
                 nc.tensor.matmul(
                     out=sc[:],
-                    lhsT=q_pairs[:, j * P : (j + 1) * P, par],
+                    lhsT=live["q_t", h][:, par, j * P : (j + 1) * P],
                     rhs=k_pairs[:, half * BANK : (half + 1) * BANK, par],
                     start=(par == 0),
                     stop=(par == 1),
@@ -132,10 +157,10 @@ def tile_heterogeneousgraphtransformer_pa_t_kernel(tc, q, k, v, adj0, adj1, out)
         def weigh(r, t, half):
             h, j = place(r, t)
             if t == 0 and half == 0:
-                live["s16", r] = work.tile([P, DUO, S], F32, bufs=4, name="s16")
+                live["sh", r] = work.tile([P, DUO, S], F32, bufs=4, name="sh")
             cols = slice(half * BANK, (half + 1) * BANK)
             nc.vector.scalar_tensor_tensor(
-                out=live["s16", r][:, t, cols],
+                out=live["sh", r][:, t, cols],
                 in0=live["adj", h][:, j, cols],
                 scalar=1e-6,
                 in1=live["sc", r, t, half][:],
@@ -143,34 +168,44 @@ def tile_heterogeneousgraphtransformer_pa_t_kernel(tc, q, k, v, adj0, adj1, out)
                 op1=ALU.mult,
             )
 
-        def mask_values(r):
+        def mask_on_scalar(r):
             h, j = place(r, 0)
-            m16 = work.tile([P, DUO, S], F32)
+            mask = work.tile([P, DUO, S], F32, bufs=3)
+            nc.scalar.activation(
+                out=mask[:, :, 0:SCALAR_COLS],
+                in_=live["adj", h][:, j : j + DUO, 0:SCALAR_COLS],
+                func=ACT.Relu,
+                bias=masked[:],
+                scale=-STEEP,
+            )
+            live["mask", r] = mask
+
+        def mask_on_vector(r):
+            h, j = place(r, 0)
             nc.vector.tensor_scalar(
-                out=m16[:],
-                in0=live["adj", h][:, j : j + DUO, :],
+                out=live["mask", r][:, :, SCALAR_COLS:S],
+                in0=live["adj", h][:, j : j + DUO, SCALAR_COLS:S],
                 scalar1=0.0,
-                scalar2=MASK / SCALE,
+                scalar2=MASKED,
                 op0=ALU.is_equal,
                 op1=ALU.mult,
             )
-            live["m16", r] = m16
 
         def add_mask(r, engine, tiles):
-            s16 = live["s16", r][:, tiles, :]
-            engine.tensor_tensor(out=s16, in0=s16, in1=live["m16", r][:, tiles, :], op=ALU.add)
+            sh = live["sh", r][:, tiles, :]
+            engine.tensor_tensor(out=sh, in0=sh, in1=live["mask", r][:, tiles, :], op=ALU.subtract)
 
         def row_max(r, tiles):
             if tiles.start == 0:
-                live["top16", r] = small.tile([P, DUO], F32, name="top16")
+                live["top", r] = small.tile([P, DUO], F32, name="top")
             nc.vector.tensor_reduce(
-                out=live["top16", r][:, tiles], in_=live["s16", r][:, tiles, :], axis=AXIS.X, op=ALU.max
+                out=live["top", r][:, tiles], in_=live["sh", r][:, tiles, :], axis=AXIS.X, op=ALU.max
             )
 
         def negate_max(r, tiles):
             if tiles.start == 0:
                 live["neg_top", r] = small.tile([P, DUO], F32, name="neg_top")
-            nc.scalar.mul(out=live["neg_top", r][:, tiles], in_=live["top16", r][:, tiles], mul=-SCALE)
+            nc.scalar.mul(out=live["neg_top", r][:, tiles], in_=live["top", r][:, tiles], mul=-UNSHRINK)
 
         def exponent(r, t):
             if t == 0:
@@ -178,10 +213,10 @@ def tile_heterogeneousgraphtransformer_pa_t_kernel(tc, q, k, v, adj0, adj1, out)
                 live["row_sum", r] = small.tile([P, DUO], F32, name="row_sum")
             nc.scalar.activation(
                 out=live["prob", r][:, t, :],
-                in_=live["s16", r][:, t, :],
+                in_=live["sh", r][:, t, :],
                 func=ACT.Exp,
                 bias=live["neg_top", r][:, t : t + 1],
-                scale=SCALE,
+                scale=UNSHRINK,
                 accum_out=live["row_sum", r][:, t : t + 1],
             )
 
@@ -298,7 +333,7 @@ def tile_heterogeneousgraphtransformer_pa_t_kernel(tc, q, k, v, adj0, adj1, out)
             run(exponent, r - 2, 1)
             prepare_heads("scalar", r)
             run(transpose_p, r - 2, 0)
-            run(mask_values, r)
+            run(mask_on_vector, r)
             run(quantise_p, r - 3, BOTH)
             run(invert_sum, r - 3)
             prepare_heads("vector", r)
@@ -310,6 +345,7 @@ def tile_heterogeneousgraphtransformer_pa_t_kernel(tc, q, k, v, adj0, adj1, out)
             run(store, r - 3, BOTH)
             run(regroup_p, r - 2, 0, nc.scalar.copy)
             run(regroup_p, r - 2, 1, nc.scalar.copy)
+            run(mask_on_scalar, r + 1)
             run(add_mask, r, nc.gpsimd, FIRST if r == LAST else BOTH)
 
         row_max(LAST - 1, BOTH)

@@ -115,8 +115,12 @@ def tile_heterogeneousgraphtransformer_pa_t_kernel(tc, q, k, v, adj0, adj1, out)
             half = piece % HALVES
             cols = slice(half * BANK, (half + 1) * BANK)
             if piece >= HALVES:
-                nc.scalar.activation(
-                    out=live["q_t", h][:, :, cols], in_=live["bank", h][:], func=ACT.Copy, scale=SHRINK
+                nc.vector.tensor_scalar(
+                    out=live["q_t", h][:, :, cols],
+                    in0=live["bank", h][:],
+                    scalar1=SHRINK,
+                    scalar2=None,
+                    op0=ALU.mult,
                 )
             else:
                 nc.scalar.copy(out=live["k_t", h][:].bitcast(F32)[:, cols], in_=live["bank", h][:])
@@ -301,7 +305,7 @@ def tile_heterogeneousgraphtransformer_pa_t_kernel(tc, q, k, v, adj0, adj1, out)
                 load_adj_v(head)
             if part == "tensor" and -5 <= rel < -1:
                 transpose_rows(head, rel + 5)
-            if part == "scalar" and -5 <= rel < -1:
+            if part == "keep" and -5 <= rel < -1:
                 keep_rows(head, rel + 5)
             if part == "scalar" and -2 <= rel < 2:
                 regroup_v(head, rel + 2)
@@ -331,6 +335,7 @@ def tile_heterogeneousgraphtransformer_pa_t_kernel(tc, q, k, v, adj0, adj1, out)
             run(negate_max, r - 2, BOTH)
             run(exponent, r - 2, 0)
             run(exponent, r - 2, 1)
+            prepare_heads("keep", r)
             prepare_heads("scalar", r)
             run(transpose_p, r - 2, 0)
             run(mask_on_vector, r)

@@ -28,7 +28,7 @@ SHRINK = 2.0**-16
 UNSHRINK = SCALE / SHRINK
 MASKED = 10000.0 / UNSHRINK
 STEEP = 3.0e38
-SCALAR_COLS = 384
+SCALAR_COLS = 448
 HEADS = E * B
 DUO = 2
 DUOS = HEADS * Q_TILES // DUO
@@ -60,70 +60,75 @@ def tile_heterogeneousgraphtransformer_pa_t_kernel(tc, q, k, v, adj0, adj1, out)
 
         live = {}
 
-        def load_qk(h):
+        def load_k(h, blocks):
             e, b = divmod(h, B)
-            k_sb = loads.tile([P, K_BLOCKS * D], BF16)
+            if blocks.start == 0:
+                live["k_sb", h] = loads.tile([P, K_BLOCKS, D], BF16, name="k_sb")
             nc.sync.dma_start(
-                out=k_sb[:].rearrange("p (t d) -> p t d", d=D), in_=k[e, b].rearrange("(t p) d -> p t d", p=P)
+                out=live["k_sb", h][:, blocks, :], in_=k[e, b].rearrange("(t p) d -> p t d", p=P)[:, blocks, :]
             )
-            q_sb = loads.tile([P, Q_TILES * D], BF16)
-            nc.sync.dma_start(out=q_sb[:], in_=q[e, b].rearrange("(p j) d -> p (j d)", j=Q_TILES))
-            live["k_sb", h], live["q_sb", h] = k_sb, q_sb
+
+        def load_q(h, tiles):
+            e, b = divmod(h, B)
+            if tiles.start == 0:
+                live["q_sb", h] = loads.tile([P, Q_TILES, D], BF16, name="q_sb")
+            nc.sync.dma_start(
+                out=live["q_sb", h][:, tiles, :], in_=q[e, b].rearrange("(p j) d -> p j d", j=Q_TILES)[:, tiles, :]
+            )
+
+        def start_head(h):
             live["k_t", h] = heads.tile([P, S * 2], BF16, name="k_t")
             live["q_t", h] = heads.tile([P, 2, S], BF16, name="q_t")
 
-        def load_adj_v(h):
+        def load_adj(h, tiles):
             e, b = divmod(h, B)
+            if tiles.start == 0:
+                live["adj", h] = loads.tile([P, Q_TILES, S], BF16, name="adj_sb")
             adj = (adj0, adj1)[e]
-            adj_sb = loads.tile([P, Q_TILES, S], BF16)
-            adj_rows = adj[b].rearrange("(p j) c -> p j c", j=Q_TILES)
-            nc.sync.dma_start(out=adj_sb[:, 0:DUO, :], in_=adj_rows[:, 0:DUO, :])
+            nc.sync.dma_start(
+                out=live["adj", h][:, tiles, :], in_=adj[b].rearrange("(p j) c -> p j c", j=Q_TILES)[:, tiles, :]
+            )
+
+        def load_v(h):
+            e, b = divmod(h, B)
             v_sb = loads.tile([P, K_BLOCKS, D], BF16)
             nc.sync.dma_start(
                 out=v_sb[:].rearrange("p (g t) d -> p g t d", t=PACK),
                 in_=v[e, b].rearrange("(g p t) d -> p g t d", p=P, t=PACK),
             )
-            for j0 in range(DUO, Q_TILES, DUO):
-                nc.sync.dma_start(out=adj_sb[:, j0 : j0 + DUO, :], in_=adj_rows[:, j0 : j0 + DUO, :])
-            live["adj", h], live["v_sb", h] = adj_sb, v_sb
+            live["v_sb", h] = v_sb
 
-        def transpose_rows(h, piece):
-            half = piece % HALVES
-            per_bank = BANK // P
-            if piece >= HALVES:
-                bank = psum_tr.tile([P, 2, BANK], BF16, tag="tr")
-                for i in range(per_bank):
-                    blk = half * per_bank + i
-                    for e in range(2):
-                        nc.tensor.transpose(
-                            bank[:, e, i * P : (i + 1) * P],
-                            live["q_sb", h][:, blk * D + e : (blk + 1) * D : 2],
-                            ident_bf[:],
-                        )
-                live["bank", h] = bank
-                return
-            words = live["k_sb", h][:].bitcast(F32)
+        def transpose_k(h, half):
+            words = live["k_sb", h][:].rearrange("p t d -> p (t d)").bitcast(F32)
             bank = psum_tr.tile([P, BANK], F32, tag="tr")
-            for i in range(per_bank):
-                blk = half * per_bank + i
+            for i in range(BANK // P):
+                blk = half * (BANK // P) + i
                 nc.tensor.transpose(
                     bank[:, i * P : (i + 1) * P], words[:, blk * WORDS : (blk + 1) * WORDS], ident_f32[:]
                 )
-            live["bank", h] = bank
+            live["k_bank", h] = bank
 
-        def keep_rows(h, piece):
-            half = piece % HALVES
+        def keep_k(h, half):
             cols = slice(half * BANK, (half + 1) * BANK)
-            if piece >= HALVES:
-                nc.vector.tensor_scalar(
-                    out=live["q_t", h][:, :, cols],
-                    in0=live["bank", h][:],
-                    scalar1=SHRINK,
-                    scalar2=None,
-                    op0=ALU.mult,
-                )
+            nc.scalar.copy(out=live["k_t", h][:].bitcast(F32)[:, cols], in_=live["k_bank", h][:])
+
+        def transpose_q(h, tiles):
+            bank = psum_tr.tile([P, 2, BANK], BF16, tag="tr")
+            for j in range(tiles.start, tiles.stop):
+                i = j - tiles.start
+                for e in range(2):
+                    nc.tensor.transpose(
+                        bank[:, e, i * P : (i + 1) * P], live["q_sb", h][:, j, e:D:2], ident_bf[:]
+                    )
+            live["q_bank", h] = bank
+
+        def keep_q(h, tiles, on_scalar=False):
+            kept = live["q_t", h][:, :, tiles.start * P : tiles.stop * P]
+            bank = live["q_bank", h][:, :, 0 : (tiles.stop - tiles.start) * P]
+            if on_scalar:
+                nc.scalar.activation(out=kept, in_=bank, func=ACT.Copy, scale=SHRINK)
             else:
-                nc.scalar.copy(out=live["k_t", h][:].bitcast(F32)[:, cols], in_=live["bank", h][:])
+                nc.vector.tensor_scalar(out=kept, in0=bank, scalar1=SHRINK, scalar2=None, op0=ALU.mult)
 
         def regroup_v(h, piece):
             if piece == 0:
@@ -299,14 +304,25 @@ def tile_heterogeneousgraphtransformer_pa_t_kernel(tc, q, k, v, adj0, adj1, out)
         def prepare(part, head, rel):
             if not 0 <= head < HEADS:
                 return
-            if part == "load" and rel == -6:
-                load_qk(head)
+            if part == "load" and rel == -5:
+                start_head(head)
+                load_k(head, slice(0, K_BLOCKS))
+                load_q(head, slice(0, Q_TILES))
             if part == "load" and rel == -4:
-                load_adj_v(head)
-            if part == "tensor" and -5 <= rel < -1:
-                transpose_rows(head, rel + 5)
-            if part == "keep" and -5 <= rel < -1:
-                keep_rows(head, rel + 5)
+                load_adj(head, slice(0, DUO))
+                load_v(head)
+                for j in range(DUO, Q_TILES, DUO):
+                    load_adj(head, slice(j, j + DUO))
+            half = rel % HALVES
+            tiles = slice(half * Q_TILES // HALVES, (half + 1) * Q_TILES // HALVES)
+            if part == "tensor" and -4 <= rel < -2:
+                transpose_k(head, half)
+            if part == "tensor" and -2 <= rel < 0:
+                transpose_q(head, tiles)
+            if part == "keep" and -4 <= rel < -2:
+                keep_k(head, half)
+            if part == "keep" and -2 <= rel < 0:
+                keep_q(head, tiles)
             if part == "scalar" and -2 <= rel < 2:
                 regroup_v(head, rel + 2)
             if part == "vector" and rel == 2:
@@ -324,7 +340,32 @@ def tile_heterogeneousgraphtransformer_pa_t_kernel(tc, q, k, v, adj0, adj1, out)
         BOTH, FIRST, SECOND = slice(0, 2), slice(0, 1), slice(1, 2)
         LAST = DUOS - 1
 
-        for r in range(-6, DUOS):
+        start_head(0)
+        load_q(0, slice(0, DUO))
+        for half in range(HALVES):
+            load_k(0, slice(half * K_BLOCKS // HALVES, (half + 1) * K_BLOCKS // HALVES))
+        load_q(0, slice(DUO, Q_TILES))
+        load_adj(0, slice(0, DUO))
+        load_v(0)
+        for j in range(DUO, Q_TILES, DUO):
+            load_adj(0, slice(j, j + DUO))
+        prepare("load", 1, -5)
+        transpose_q(0, slice(0, DUO))
+        keep_q(0, slice(0, DUO))
+        for half in range(HALVES):
+            transpose_k(0, half)
+            keep_k(0, half)
+            scores(0, 0, half)
+        for half in range(HALVES):
+            scores(0, 1, half)
+        for tiles in (slice(DUO, DUO + 4), slice(DUO + 4, Q_TILES)):
+            transpose_q(0, tiles)
+            keep_q(0, tiles, on_scalar=True)
+        mask_on_scalar(0)
+        regroup_v(0, 0)
+        regroup_v(0, 1)
+
+        for r in range(DUOS):
             prepare_heads("load", r)
             for t in range(DUO):
                 for half in range(HALVES):
@@ -335,13 +376,13 @@ def tile_heterogeneousgraphtransformer_pa_t_kernel(tc, q, k, v, adj0, adj1, out)
             run(negate_max, r - 2, BOTH)
             run(exponent, r - 2, 0)
             run(exponent, r - 2, 1)
-            prepare_heads("keep", r)
             prepare_heads("scalar", r)
             run(transpose_p, r - 2, 0)
+            prepare_heads("vector", r)
             run(mask_on_vector, r)
             run(quantise_p, r - 3, BOTH)
             run(invert_sum, r - 3)
-            prepare_heads("vector", r)
+            prepare_heads("keep", r)
             run(weighted_sum, r - 3, 0, psum_o, "acc")
             run(weighted_sum, r - 3, 1, psum_o, "acc")
             run(transpose_p, r - 2, 1)

@@ -28,7 +28,8 @@ SHRINK = 2.0**-16
 UNSHRINK = SCALE / SHRINK
 MASKED = 10000.0 / UNSHRINK
 STEEP = 3.0e38
-SCALAR_COLS = 448
+SHRUNK_BY_MATMUL = 6
+SCALAR_COLS = 256
 HEADS = E * B
 DUO = 2
 DUOS = HEADS * Q_TILES // DUO
@@ -55,6 +56,10 @@ def tile_heterogeneousgraphtransformer_pa_t_kernel(tc, q, k, v, adj0, adj1, out)
 
         ident_bf = consts.tile([P, P], BF16)
         make_identity(nc, ident_bf[:])
+        shrink_ident = consts.tile([P, P], BF16)
+        nc.vector.tensor_scalar(
+            out=shrink_ident[:], in0=ident_bf[:], scalar1=SHRINK, scalar2=None, op0=ALU.mult
+        )
         masked = consts.tile([P, 1], F32)
         nc.vector.memset(masked[:], MASKED)
 
@@ -106,37 +111,41 @@ def tile_heterogeneousgraphtransformer_pa_t_kernel(tc, q, k, v, adj0, adj1, out)
                 nc.tensor.transpose(
                     bank[:, i * P : (i + 1) * P], words[:, blk * WORDS : (blk + 1) * WORDS], ident_f32[:]
                 )
-            live["k_bank", h] = bank
+            live["k_bank", h, half] = bank
 
         def keep_k(h, half):
             cols = slice(half * BANK, (half + 1) * BANK)
-            nc.scalar.copy(out=live["k_t", h][:].bitcast(F32)[:, cols], in_=live["k_bank", h][:])
+            nc.scalar.copy(out=live["k_t", h][:].bitcast(F32)[:, cols], in_=live["k_bank", h, half][:])
 
         def transpose_q(h, tiles):
             bank = psum_tr.tile([P, 2, BANK], BF16, tag="tr")
             for j in range(tiles.start, tiles.stop):
                 i = j - tiles.start
                 for e in range(2):
-                    nc.tensor.transpose(
-                        bank[:, e, i * P : (i + 1) * P], live["q_sb", h][:, j, e:D:2], ident_bf[:]
-                    )
+                    turned = bank[:, e, i * P : (i + 1) * P]
+                    rows = live["q_sb", h][:, j, e:D:2]
+                    if j < SHRUNK_BY_MATMUL:
+                        nc.tensor.matmul(out=turned, lhsT=rows, rhs=shrink_ident[:], start=True, stop=True)
+                    else:
+                        nc.tensor.transpose(turned, rows, ident_bf[:])
             live["q_bank", h] = bank
 
-        def keep_q(h, tiles, on_scalar=False):
-            kept = live["q_t", h][:, :, tiles.start * P : tiles.stop * P]
-            bank = live["q_bank", h][:, :, 0 : (tiles.stop - tiles.start) * P]
-            if on_scalar:
-                nc.scalar.activation(out=kept, in_=bank, func=ACT.Copy, scale=SHRINK)
-            else:
-                nc.vector.tensor_scalar(out=kept, in0=bank, scalar1=SHRINK, scalar2=None, op0=ALU.mult)
+        def keep_q(h, tiles):
+            nc.scalar.copy(
+                out=live["q_t", h][:, :, tiles.start * P : tiles.stop * P],
+                in_=live["q_bank", h][:, :, 0 : (tiles.stop - tiles.start) * P],
+            )
+
+        def shrink_q(h):
+            q_rows = live["q_sb", h][:, SHRUNK_BY_MATMUL:Q_TILES, :]
+            nc.vector.tensor_scalar(out=q_rows, in0=q_rows, scalar1=SHRINK, scalar2=None, op0=ALU.mult)
 
         def regroup_v(h, piece):
             if piece == 0:
                 live["v_grouped", h] = heads.tile([P, PASSES * D * PACK], BF16, align_bytes=64, name="v_grouped")
-            g, cols = piece // 2, slice((piece % 2) * P, (piece % 2 + 1) * P)
             nc.scalar.copy(
-                out=live["v_grouped", h][:].rearrange("p (g d t) -> p g d t", g=PASSES, t=PACK)[:, g, cols, :],
-                in_=live["v_sb", h][:].rearrange("p (g t) d -> p g d t", t=PACK)[:, g, cols, :],
+                out=live["v_grouped", h][:].rearrange("p (g d t) -> p g d t", g=PASSES, t=PACK)[:, piece],
+                in_=live["v_sb", h][:].rearrange("p (g t) d -> p g d t", t=PACK)[:, piece],
             )
 
         def quantise_v(h):
@@ -287,7 +296,7 @@ def tile_heterogeneousgraphtransformer_pa_t_kernel(tc, q, k, v, adj0, adj1, out)
 
         def normalise(r, t):
             if t == 0:
-                live["o_sb", r] = work.tile([P, DUO, D], F32, name="o_sb")
+                live["o_sb", r] = work.tile([P, DUO, D], F32, bufs=4, name="o_sb")
             nc.scalar.activation(
                 out=live["o_sb", r][:, t, :],
                 in_=live["acc", r][:, t * D : (t + 1) * D],
@@ -323,8 +332,10 @@ def tile_heterogeneousgraphtransformer_pa_t_kernel(tc, q, k, v, adj0, adj1, out)
                 keep_k(head, half)
             if part == "keep" and -2 <= rel < 0:
                 keep_q(head, tiles)
-            if part == "scalar" and -2 <= rel < 2:
-                regroup_v(head, rel + 2)
+            if part == "scalar" and 0 <= rel < 2:
+                regroup_v(head, rel)
+            if part == "vector" and rel == -3:
+                shrink_q(head)
             if part == "vector" and rel == 2:
                 quantise_v(head)
 
@@ -344,8 +355,9 @@ def tile_heterogeneousgraphtransformer_pa_t_kernel(tc, q, k, v, adj0, adj1, out)
         load_q(0, slice(0, DUO))
         for half in range(HALVES):
             load_k(0, slice(half * K_BLOCKS // HALVES, (half + 1) * K_BLOCKS // HALVES))
+        load_adj(0, slice(0, 1))
         load_q(0, slice(DUO, Q_TILES))
-        load_adj(0, slice(0, DUO))
+        load_adj(0, slice(1, DUO))
         load_v(0)
         for j in range(DUO, Q_TILES, DUO):
             load_adj(0, slice(j, j + DUO))
@@ -355,15 +367,14 @@ def tile_heterogeneousgraphtransformer_pa_t_kernel(tc, q, k, v, adj0, adj1, out)
         for half in range(HALVES):
             transpose_k(0, half)
             keep_k(0, half)
-            scores(0, 0, half)
-        for half in range(HALVES):
-            scores(0, 1, half)
-        for tiles in (slice(DUO, DUO + 4), slice(DUO + 4, Q_TILES)):
-            transpose_q(0, tiles)
-            keep_q(0, tiles, on_scalar=True)
+        for t in range(DUO):
+            for half in range(HALVES):
+                scores(0, t, half)
         mask_on_scalar(0)
-        regroup_v(0, 0)
-        regroup_v(0, 1)
+        shrink_q(0)
+        for tiles in (slice(DUO, SHRUNK_BY_MATMUL), slice(SHRUNK_BY_MATMUL, Q_TILES)):
+            transpose_q(0, tiles)
+            keep_q(0, tiles)
 
         for r in range(DUOS):
             prepare_heads("load", r)
@@ -376,13 +387,13 @@ def tile_heterogeneousgraphtransformer_pa_t_kernel(tc, q, k, v, adj0, adj1, out)
             run(negate_max, r - 2, BOTH)
             run(exponent, r - 2, 0)
             run(exponent, r - 2, 1)
+            prepare_heads("keep", r)
             prepare_heads("scalar", r)
             run(transpose_p, r - 2, 0)
             prepare_heads("vector", r)
             run(mask_on_vector, r)
             run(quantise_p, r - 3, BOTH)
             run(invert_sum, r - 3)
-            prepare_heads("keep", r)
             run(weighted_sum, r - 3, 0, psum_o, "acc")
             run(weighted_sum, r - 3, 1, psum_o, "acc")
             run(transpose_p, r - 2, 1)

@@ -29,6 +29,7 @@ UNSHRINK = SCALE / SHRINK
 MASKED = 10000.0 / UNSHRINK
 STEEP = 3.0e38
 SHRUNK_BY_MATMUL = 6
+VECTOR_COLS = 32
 SCALAR_COLS = 256
 HEADS = E * B
 DUO = 2
@@ -186,32 +187,32 @@ def tile_heterogeneousgraphtransformer_pa_t_kernel(tc, q, k, v, adj0, adj1, out)
                 op1=ALU.mult,
             )
 
-        def mask_on_scalar(r):
+        def mask_on_scalar(r, tiles):
             h, j = place(r, 0)
-            mask = work.tile([P, DUO, S], F32, bufs=3)
+            if tiles.start == 0:
+                live["mask", r] = work.tile([P, DUO, S], F32, bufs=3, name="mask")
             nc.scalar.activation(
-                out=mask[:, :, 0:SCALAR_COLS],
-                in_=live["adj", h][:, j : j + DUO, 0:SCALAR_COLS],
+                out=live["mask", r][:, tiles, 0:SCALAR_COLS],
+                in_=live["adj", h][:, j + tiles.start : j + tiles.stop, 0:SCALAR_COLS],
                 func=ACT.Relu,
                 bias=masked[:],
                 scale=-STEEP,
             )
-            live["mask", r] = mask
 
-        def mask_on_vector(r):
+        def mask_on_vector(r, tiles):
             h, j = place(r, 0)
             nc.vector.tensor_scalar(
-                out=live["mask", r][:, :, SCALAR_COLS:S],
-                in0=live["adj", h][:, j : j + DUO, SCALAR_COLS:S],
+                out=live["mask", r][:, tiles, SCALAR_COLS:S],
+                in0=live["adj", h][:, j + tiles.start : j + tiles.stop, SCALAR_COLS:S],
                 scalar1=0.0,
                 scalar2=MASKED,
                 op0=ALU.is_equal,
                 op1=ALU.mult,
             )
 
-        def add_mask(r, engine, tiles):
-            sh = live["sh", r][:, tiles, :]
-            engine.tensor_tensor(out=sh, in0=sh, in1=live["mask", r][:, tiles, :], op=ALU.subtract)
+        def add_mask(r, tiles, engine=nc.gpsimd, cols=slice(0, S - VECTOR_COLS)):
+            sh = live["sh", r][:, tiles, cols]
+            engine.tensor_tensor(out=sh, in0=sh, in1=live["mask", r][:, tiles, cols], op=ALU.subtract)
 
         def row_max(r, tiles):
             if tiles.start == 0:
@@ -334,7 +335,7 @@ def tile_heterogeneousgraphtransformer_pa_t_kernel(tc, q, k, v, adj0, adj1, out)
                 keep_q(head, tiles)
             if part == "scalar" and 0 <= rel < 2:
                 regroup_v(head, rel)
-            if part == "vector" and rel == -3:
+            if part == "vector" and rel == -2:
                 shrink_q(head)
             if part == "vector" and rel == 2:
                 quantise_v(head)
@@ -358,30 +359,43 @@ def tile_heterogeneousgraphtransformer_pa_t_kernel(tc, q, k, v, adj0, adj1, out)
         load_adj(0, slice(0, 1))
         load_q(0, slice(DUO, Q_TILES))
         load_adj(0, slice(1, DUO))
+        load_adj(0, slice(DUO, 2 * DUO))
+        start_head(1)
+        load_k(1, slice(0, K_BLOCKS))
         load_v(0)
-        for j in range(DUO, Q_TILES, DUO):
+        for j in range(2 * DUO, Q_TILES, DUO):
             load_adj(0, slice(j, j + DUO))
-        prepare("load", 1, -5)
+        load_q(1, slice(0, Q_TILES))
         transpose_q(0, slice(0, DUO))
         keep_q(0, slice(0, DUO))
         for half in range(HALVES):
             transpose_k(0, half)
             keep_k(0, half)
-        for t in range(DUO):
+        for tiles in (FIRST, SECOND):
+            mask_on_scalar(0, tiles)
+            mask_on_vector(0, tiles)
             for half in range(HALVES):
-                scores(0, t, half)
-        mask_on_scalar(0)
-        shrink_q(0)
-        for tiles in (slice(DUO, SHRUNK_BY_MATMUL), slice(SHRUNK_BY_MATMUL, Q_TILES)):
-            transpose_q(0, tiles)
-            keep_q(0, tiles)
+                scores(0, tiles.start, half)
+                weigh(0, tiles.start, half)
+            add_mask(0, tiles, cols=slice(0, S))
+            if tiles == FIRST:
+                transpose_q(0, slice(DUO, 2 * DUO))
+                keep_q(0, slice(DUO, 2 * DUO))
+                shrink_q(0)
+            else:
+                mask_on_scalar(1, BOTH)
 
         for r in range(DUOS):
             prepare_heads("load", r)
             for t in range(DUO):
                 for half in range(HALVES):
-                    run(weigh, r, t, half)
+                    if r > 0:
+                        weigh(r, t, half)
                     run(scores, r + 1, t, half)
+            if r == 0:
+                for tiles in (slice(2 * DUO, SHRUNK_BY_MATMUL), slice(SHRUNK_BY_MATMUL, Q_TILES)):
+                    transpose_q(0, tiles)
+                    keep_q(0, tiles)
             prepare_heads("tensor", r)
             run(row_max, r - 2, BOTH)
             run(negate_max, r - 2, BOTH)
@@ -391,8 +405,11 @@ def tile_heterogeneousgraphtransformer_pa_t_kernel(tc, q, k, v, adj0, adj1, out)
             prepare_heads("scalar", r)
             run(transpose_p, r - 2, 0)
             prepare_heads("vector", r)
-            run(mask_on_vector, r)
+            if r > 0:
+                mask_on_vector(r, BOTH)
             run(quantise_p, r - 3, BOTH)
+            if r > 0:
+                add_mask(r, BOTH, nc.vector, slice(S - VECTOR_COLS, S))
             run(invert_sum, r - 3)
             run(weighted_sum, r - 3, 0, psum_o, "acc")
             run(weighted_sum, r - 3, 1, psum_o, "acc")
@@ -400,14 +417,18 @@ def tile_heterogeneousgraphtransformer_pa_t_kernel(tc, q, k, v, adj0, adj1, out)
             run(normalise, r - 3, 0)
             run(normalise, r - 3, 1)
             run(store, r - 3, BOTH)
-            run(regroup_p, r - 2, 0, nc.scalar.copy)
-            run(regroup_p, r - 2, 1, nc.scalar.copy)
-            run(mask_on_scalar, r + 1)
-            run(add_mask, r, nc.gpsimd, FIRST if r == LAST else BOTH)
+            if r < LAST:
+                run(regroup_p, r - 2, 0, nc.scalar.copy)
+                run(regroup_p, r - 2, 1, nc.scalar.copy)
+            if r > 0:
+                run(mask_on_scalar, r + 1, BOTH)
+            for tiles in () if r == 0 else (FIRST, SECOND) if r == LAST else (BOTH,):
+                add_mask(r, tiles)
 
         row_max(LAST - 1, BOTH)
         row_max(LAST, FIRST)
-        add_mask(LAST, nc.vector, SECOND)
+        for t in range(DUO):
+            regroup_p(LAST - 2, t, nc.vector.tensor_copy)
         row_max(LAST, SECOND)
         quantise_p(LAST - 2, BOTH)
         invert_sum(LAST - 2)

@@ -15,6 +15,7 @@ AXIS = mybir.AxisListType
 E, B, S, D = 2, 4, 1024, 256
 P = 128
 PACK = 4
+RUN = 4
 PAIRS = PACK // 2
 K_PASS = P * PACK
 PASSES = S // K_PASS
@@ -30,7 +31,7 @@ MASKED = 10000.0 / UNSHRINK
 STEEP = 3.0e38
 SHRUNK_BY_MATMUL = 6
 VECTOR_COLS = 32
-SCALAR_COLS = 256
+SCALAR_COLS = 288
 HEADS = E * B
 DUO = 2
 DUOS = HEADS * Q_TILES // DUO
@@ -145,8 +146,8 @@ def tile_heterogeneousgraphtransformer_pa_t_kernel(tc, q, k, v, adj0, adj1, out)
             if piece == 0:
                 live["v_grouped", h] = heads.tile([P, PASSES * D * PACK], BF16, align_bytes=64, name="v_grouped")
             nc.scalar.copy(
-                out=live["v_grouped", h][:].rearrange("p (g d t) -> p g d t", g=PASSES, t=PACK)[:, piece],
-                in_=live["v_sb", h][:].rearrange("p (g t) d -> p g d t", t=PACK)[:, piece],
+                out=live["v_grouped", h][:].rearrange("p (g c i t) -> p g c t i", g=PASSES, i=RUN, t=PACK)[:, piece],
+                in_=live["v_sb", h][:].rearrange("p (g t) (c i) -> p g c t i", t=PACK, i=RUN)[:, piece],
             )
 
         def quantise_v(h):

@@ -30,8 +30,8 @@ UNSHRINK = SCALE / SHRINK
 MASKED = 10000.0 / UNSHRINK
 STEEP = 3.0e38
 SHRUNK_BY_MATMUL = 6
-VECTOR_COLS = 32
-SCALAR_COLS = 288
+VECTOR_COLS = 48
+SCALAR_COLS = 224
 HEADS = E * B
 DUO = 2
 DUOS = HEADS * Q_TILES // DUO
@@ -133,14 +133,20 @@ def tile_heterogeneousgraphtransformer_pa_t_kernel(tc, q, k, v, adj0, adj1, out)
             live["q_bank", h] = bank
 
         def keep_q(h, tiles):
-            nc.scalar.copy(
-                out=live["q_t", h][:, :, tiles.start * P : tiles.stop * P],
-                in_=live["q_bank", h][:, :, 0 : (tiles.stop - tiles.start) * P],
-            )
-
-        def shrink_q(h):
-            q_rows = live["q_sb", h][:, SHRUNK_BY_MATMUL:Q_TILES, :]
-            nc.vector.tensor_scalar(out=q_rows, in0=q_rows, scalar1=SHRINK, scalar2=None, op0=ALU.mult)
+            shrunk = min(tiles.stop, SHRUNK_BY_MATMUL)
+            kept, bank = live["q_t", h], live["q_bank", h]
+            if tiles.start < shrunk:
+                nc.scalar.copy(
+                    out=kept[:, :, tiles.start * P : shrunk * P], in_=bank[:, :, 0 : (shrunk - tiles.start) * P]
+                )
+            if shrunk < tiles.stop:
+                first = max(tiles.start, shrunk)
+                nc.scalar.activation(
+                    out=kept[:, :, first * P : tiles.stop * P],
+                    in_=bank[:, :, (first - tiles.start) * P : (tiles.stop - tiles.start) * P],
+                    func=ACT.Copy,
+                    scale=SHRINK,
+                )
 
         def regroup_v(h, piece):
             if piece == 0:
@@ -336,8 +342,6 @@ def tile_heterogeneousgraphtransformer_pa_t_kernel(tc, q, k, v, adj0, adj1, out)
                 keep_q(head, tiles)
             if part == "scalar" and 0 <= rel < 2:
                 regroup_v(head, rel)
-            if part == "vector" and rel == -2:
-                shrink_q(head)
             if part == "vector" and rel == 2:
                 quantise_v(head)
 
@@ -382,7 +386,6 @@ def tile_heterogeneousgraphtransformer_pa_t_kernel(tc, q, k, v, adj0, adj1, out)
             if tiles == FIRST:
                 transpose_q(0, slice(DUO, 2 * DUO))
                 keep_q(0, slice(DUO, 2 * DUO))
-                shrink_q(0)
             else:
                 mask_on_scalar(1, BOTH)
 

from contextlib import ExitStack

import concourse.mybir as mybir
from concourse.masks import make_identity

F32 = mybir.dt.float32
BF16 = mybir.dt.bfloat16
U32 = mybir.dt.uint32
U8 = mybir.dt.uint8
FP8X4 = mybir.dt.float8_e4m3fn_x4
ALU = mybir.AluOpType
ACT = mybir.ActivationFunctionType
AXIS = mybir.AxisListType

E, B, S, D = 2, 4, 1024, 256
P = 128
PACK = 4
RUN = 4
PAIRS = PACK // 2
K_PASS = P * PACK
PASSES = S // K_PASS
Q_TILES = S // P
K_BLOCKS = S // P
BANK = 512
HALVES = S // BANK
WORDS = D // 2
SCALE = 1.0 / 16.0
SHRINK = 2.0**-16
UNSHRINK = SCALE / SHRINK
MASKED = 10000.0 / UNSHRINK
STEEP = 3.0e38
SHRUNK_BY_MATMUL = 6
VECTOR_COLS = 48
SCALAR_COLS = 224
HEADS = E * B
DUO = 2
DUOS = HEADS * Q_TILES // DUO
HEAD_DUOS = Q_TILES // DUO

FLOPS = 2 * (2 * E * B * S * S * D)


def tile_heterogeneousgraphtransformer_pa_t_kernel(tc, q, k, v, adj0, adj1, out):
    nc = tc.nc
    with ExitStack() as ctx:
        consts = ctx.enter_context(tc.tile_pool(name="consts", bufs=1))
        loads = ctx.enter_context(tc.tile_pool(name="loads", bufs=2))
        heads = ctx.enter_context(tc.tile_pool(name="heads", bufs=2))
        work = ctx.enter_context(tc.tile_pool(name="work", bufs=2))
        small = ctx.enter_context(tc.tile_pool(name="small", bufs=4))
        psum_sc = ctx.enter_context(tc.psum_pool(name="psum_sc", bufs=DUO * HALVES))
        psum_tr = ctx.enter_context(tc.psum_pool(name="psum_tr", bufs=3))
        psum_o = ctx.enter_context(tc.psum_pool(name="psum_o", bufs=1))
        ctx.enter_context(tc.manual_schedule())

        ident_f32 = consts.tile([P, P], F32)
        make_identity(nc, ident_f32[:])

        ident_bf = consts.tile([P, P], BF16)
        make_identity(nc, ident_bf[:])
        shrink_ident = consts.tile([P, P], BF16)
        nc.vector.tensor_scalar(
            out=shrink_ident[:], in0=ident_bf[:], scalar1=SHRINK, scalar2=None, op0=ALU.mult
        )
        masked = consts.tile([P, 1], F32)
        nc.vector.memset(masked[:], MASKED)

        live = {}

        def load_k(h, blocks):
            e, b = divmod(h, B)
            if blocks.start == 0:
                live["k_sb", h] = loads.tile([P, K_BLOCKS, D], BF16, name="k_sb")
            nc.sync.dma_start(
                out=live["k_sb", h][:, blocks, :], in_=k[e, b].rearrange("(t p) d -> p t d", p=P)[:, blocks, :]
            )

        def load_q(h, tiles):
            e, b = divmod(h, B)
            if tiles.start == 0:
                live["q_sb", h] = loads.tile([P, Q_TILES, D], BF16, name="q_sb")
            nc.sync.dma_start(
                out=live["q_sb", h][:, tiles, :], in_=q[e, b].rearrange("(p j) d -> p j d", j=Q_TILES)[:, tiles, :]
            )

        def start_head(h):
            live["k_t", h] = heads.tile([P, S * 2], BF16, name="k_t")
            live["q_t", h] = heads.tile([P, 2, S], BF16, name="q_t")

        def load_adj(h, tiles):
            e, b = divmod(h, B)
            if tiles.start == 0:
                live["adj", h] = loads.tile([P, Q_TILES, S], BF16, name="adj_sb")
            adj = (adj0, adj1)[e]
            nc.sync.dma_start(
                out=live["adj", h][:, tiles, :], in_=adj[b].rearrange("(p j) c -> p j c", j=Q_TILES)[:, tiles, :]
            )

        def load_v(h):
            e, b = divmod(h, B)
            v_sb = loads.tile([P, K_BLOCKS, D], BF16)
            nc.sync.dma_start(
                out=v_sb[:].rearrange("p (g t) d -> p g t d", t=PACK),
                in_=v[e, b].rearrange("(g p t) d -> p g t d", p=P, t=PACK),
            )
            live["v_sb", h] = v_sb

        def transpose_k(h, half):
            words = live["k_sb", h][:].rearrange("p t d -> p (t d)").bitcast(F32)
            bank = psum_tr.tile([P, BANK], F32, tag="tr")
            for i in range(BANK // P):
                blk = half * (BANK // P) + i
                nc.tensor.transpose(
                    bank[:, i * P : (i + 1) * P], words[:, blk * WORDS : (blk + 1) * WORDS], ident_f32[:]
                )
            live["k_bank", h, half] = bank

        def keep_k(h, half):
            cols = slice(half * BANK, (half + 1) * BANK)
            nc.scalar.copy(out=live["k_t", h][:].bitcast(F32)[:, cols], in_=live["k_bank", h, half][:])

        def transpose_q(h, tiles):
            bank = psum_tr.tile([P, 2, BANK], BF16, tag="tr")
            for j in range(tiles.start, tiles.stop):
                i = j - tiles.start
                for e in range(2):
                    turned = bank[:, e, i * P : (i + 1) * P]
                    rows = live["q_sb", h][:, j, e:D:2]
                    if j < SHRUNK_BY_MATMUL:
                        nc.tensor.matmul(out=turned, lhsT=rows, rhs=shrink_ident[:], start=True, stop=True)
                    else:
                        nc.tensor.transpose(turned, rows, ident_bf[:])
            live["q_bank", h] = bank

        def keep_q(h, tiles):
            shrunk = min(tiles.stop, SHRUNK_BY_MATMUL)
            kept, bank = live["q_t", h], live["q_bank", h]
            if tiles.start < shrunk:
                nc.scalar.copy(
                    out=kept[:, :, tiles.start * P : shrunk * P], in_=bank[:, :, 0 : (shrunk - tiles.start) * P]
                )
            if shrunk < tiles.stop:
                first = max(tiles.start, shrunk)
                nc.scalar.activation(
                    out=kept[:, :, first * P : tiles.stop * P],
                    in_=bank[:, :, (first - tiles.start) * P : (tiles.stop - tiles.start) * P],
                    func=ACT.Copy,
                    scale=SHRINK,
                )

        def regroup_v(h, piece):
            if piece == 0:
                live["v_grouped", h] = heads.tile([P, PASSES * D * PACK], BF16, align_bytes=64, name="v_grouped")
            nc.scalar.copy(
                out=live["v_grouped", h][:].rearrange("p (g c i t) -> p g c t i", g=PASSES, i=RUN, t=PACK)[:, piece],
                in_=live["v_sb", h][:].rearrange("p (g t) (c i) -> p g c t i", t=PACK, i=RUN)[:, piece],
            )

        def quantise_v(h):
            v_codes = heads.tile([P, PASSES * D], U32, align_bytes=64)
            v_scales = heads.tile([P, PASSES * D], U8, align_bytes=64)
            nc.vector.quantize_mx(out=v_codes[:].bitcast(FP8X4), scales=v_scales[:], in_=live["v_grouped", h][:])
            live["v_codes", h], live["v_scales", h] = v_codes, v_scales

        def place(r, t):
            h, d = divmod(r, HEAD_DUOS)
            return h, d * DUO + t

        def scores(r, t, half):
            h, j = place(r, t)
            k_pairs = live["k_t", h][:].rearrange("w (c e) -> w c e", e=2)
            sc = psum_sc.tile([P, BANK], F32, tag="sc")
            for par in range(2):
                nc.tensor.matmul(
                    out=sc[:],
                    lhsT=live["q_t", h][:, par, j * P : (j + 1) * P],
                    rhs=k_pairs[:, half * BANK : (half + 1) * BANK, par],
                    start=(par == 0),
                    stop=(par == 1),
                )
            live["sc", r, t, half] = sc

        def weigh(r, t, half):
            h, j = place(r, t)
            if t == 0 and half == 0:
                live["sh", r] = work.tile([P, DUO, S], F32, bufs=4, name="sh")
            cols = slice(half * BANK, (half + 1) * BANK)
            nc.vector.scalar_tensor_tensor(
                out=live["sh", r][:, t, cols],
                in0=live["adj", h][:, j, cols],
                scalar=1e-6,
                in1=live["sc", r, t, half][:],
                op0=ALU.add,
                op1=ALU.mult,
            )

        def mask_on_scalar(r, tiles):
            h, j = place(r, 0)
            if tiles.start == 0:
                live["mask", r] = work.tile([P, DUO, S], F32, bufs=3, name="mask")
            nc.scalar.activation(
                out=live["mask", r][:, tiles, 0:SCALAR_COLS],
                in_=live["adj", h][:, j + tiles.start : j + tiles.stop, 0:SCALAR_COLS],
                func=ACT.Relu,
                bias=masked[:],
                scale=-STEEP,
            )

        def mask_on_vector(r, tiles):
            h, j = place(r, 0)
            nc.vector.tensor_scalar(
                out=live["mask", r][:, tiles, SCALAR_COLS:S],
                in0=live["adj", h][:, j + tiles.start : j + tiles.stop, SCALAR_COLS:S],
                scalar1=0.0,
                scalar2=MASKED,
                op0=ALU.is_equal,
                op1=ALU.mult,
            )

        def add_mask(r, tiles, engine=nc.gpsimd, cols=slice(0, S - VECTOR_COLS)):
            sh = live["sh", r][:, tiles, cols]
            engine.tensor_tensor(out=sh, in0=sh, in1=live["mask", r][:, tiles, cols], op=ALU.subtract)

        def row_max(r, tiles):
            if tiles.start == 0:
                live["top", r] = small.tile([P, DUO], F32, name="top")
            nc.vector.tensor_reduce(
                out=live["top", r][:, tiles], in_=live["sh", r][:, tiles, :], axis=AXIS.X, op=ALU.max
            )

        def negate_max(r, tiles):
            if tiles.start == 0:
                live["neg_top", r] = small.tile([P, DUO], F32, name="neg_top")
            nc.scalar.mul(out=live["neg_top", r][:, tiles], in_=live["top", r][:, tiles], mul=-UNSHRINK)

        def exponent(r, t):
            if t == 0:
                live["prob", r] = work.tile([P, DUO, S], BF16, name="prob")
                live["row_sum", r] = small.tile([P, DUO], F32, name="row_sum")
            nc.scalar.activation(
                out=live["prob", r][:, t, :],
                in_=live["sh", r][:, t, :],
                func=ACT.Exp,
                bias=live["neg_top", r][:, t : t + 1],
                scale=UNSHRINK,
                accum_out=live["row_sum", r][:, t : t + 1],
            )

        def transpose_p(r, t):
            words = live["prob", r][:].rearrange("p t c -> p (t c)").bitcast(F32)
            first = t * S // 2
            prob_t = psum_tr.tile([P, BANK], F32, tag="tr")
            for g in range(PASSES):
                for u in range(PAIRS):
                    blk = PAIRS * g + u
                    nc.tensor.transpose(
                        prob_t[:, blk * P : (blk + 1) * P],
                        words[:, first + g * PAIRS * P + u : first + (g + 1) * PAIRS * P : PAIRS],
                        ident_f32[:],
                    )
            live["prob_t", r, t] = prob_t

        def regroup_p(r, t, copy):
            if t == 0:
                live["p_grouped", r] = work.tile([P, DUO * S], BF16, align_bytes=64, name="p_grouped")
            copy(
                out=live["p_grouped", r][:, t * S : (t + 1) * S]
                .bitcast(F32)
                .rearrange("p (g r u) -> p g r u", g=PASSES, u=PAIRS),
                in_=live["prob_t", r, t][:].rearrange("p (g u r) -> p g r u", g=PASSES, u=PAIRS),
            )

        def quantise_p(r, tiles):
            if tiles.start == 0:
                live["p_codes", r] = work.tile([P, DUO * PASSES * P], U32, align_bytes=64, name="p_codes")
                live["p_scales", r] = work.tile([P, DUO * PASSES * P], U8, align_bytes=64, name="p_scales")
            words = slice(tiles.start * PASSES * P, tiles.stop * PASSES * P)
            nc.vector.quantize_mx(
                out=live["p_codes", r][:, words].bitcast(FP8X4),
                scales=live["p_scales", r][:, words],
                in_=live["p_grouped", r][:, tiles.start * S : tiles.stop * S],
            )

        def weighted_sum(r, t, pool, tag):
            h = r // HEAD_DUOS
            if t == 0:
                live["acc", r] = pool.tile([P, DUO * D], F32, tag=tag, name="acc")
            for g in range(PASSES):
                words = slice((t * PASSES + g) * P, (t * PASSES + g + 1) * P)
                nc.tensor.matmul_mx(
                    out=live["acc", r][:, t * D : (t + 1) * D],
                    lhsT=live["p_codes", r][:, words].bitcast(FP8X4),
                    lhsT_scale=live["p_scales", r][:, words],
                    rhs=live["v_codes", h][:, g * D : (g + 1) * D].bitcast(FP8X4),
                    rhs_scale=live["v_scales", h][:, g * D : (g + 1) * D],
                    start=(g == 0),
                    stop=(g == PASSES - 1),
                )

        def invert_sum(r):
            inv_sum = small.tile([P, DUO], F32)
            nc.vector.reciprocal(out=inv_sum[:], in_=live["row_sum", r][:])
            live["inv_sum", r] = inv_sum

        def normalise(r, t):
            if t == 0:
                live["o_sb", r] = work.tile([P, DUO, D], F32, bufs=4, name="o_sb")
            nc.scalar.activation(
                out=live["o_sb", r][:, t, :],
                in_=live["acc", r][:, t * D : (t + 1) * D],
                func=ACT.Copy,
                scale=live["inv_sum", r][:, t : t + 1],
            )

        def store(r, tiles):
            h, j = place(r, 0)
            e, b = divmod(h, B)
            rows = out[e, b].rearrange("(p j) d -> p j d", j=Q_TILES)
            nc.sync.dma_start(out=rows[:, j + tiles.start : j + tiles.stop, :], in_=live["o_sb", r][:, tiles, :])

        def prepare(part, head, rel):
            if not 0 <= head < HEADS:
                return
            if part == "load" and rel == -5:
                start_head(head)
                load_k(head, slice(0, K_BLOCKS))
                load_q(head, slice(0, Q_TILES))
            if part == "load" and rel == -4:
                load_adj(head, slice(0, DUO))
                load_v(head)
                for j in range(DUO, Q_TILES, DUO):
                    load_adj(head, slice(j, j + DUO))
            half = rel % HALVES
            tiles = slice(half * Q_TILES // HALVES, (half + 1) * Q_TILES // HALVES)
            if part == "tensor" and -4 <= rel < -2:
                transpose_k(head, half)
            if part == "tensor" and -2 <= rel < 0:
                transpose_q(head, tiles)
            if part == "keep" and -4 <= rel < -2:
                keep_k(head, half)
            if part == "keep" and -2 <= rel < 0:
                keep_q(head, tiles)
            if part == "scalar" and 0 <= rel < 2:
                regroup_v(head, rel)
            if part == "vector" and rel == 2:
                quantise_v(head)

        def prepare_heads(part, r):
            now = r // HEAD_DUOS
            for head in (now + 2, now + 1, now):
                prepare(part, head, r - head * HEAD_DUOS)

        def run(stage, r, *more):
            if 0 <= r < DUOS:
                stage(r, *more)

        BOTH, FIRST, SECOND = slice(0, 2), slice(0, 1), slice(1, 2)
        LAST = DUOS - 1

        start_head(0)
        load_q(0, slice(0, DUO))
        for half in range(HALVES):
            load_k(0, slice(half * K_BLOCKS // HALVES, (half + 1) * K_BLOCKS // HALVES))
        load_adj(0, slice(0, 1))
        load_q(0, slice(DUO, Q_TILES))
        load_adj(0, slice(1, DUO))
        load_adj(0, slice(DUO, 2 * DUO))
        start_head(1)
        load_k(1, slice(0, K_BLOCKS))
        load_v(0)
        for j in range(2 * DUO, Q_TILES, DUO):
            load_adj(0, slice(j, j + DUO))
        load_q(1, slice(0, Q_TILES))
        transpose_q(0, slice(0, DUO))
        keep_q(0, slice(0, DUO))
        for half in range(HALVES):
            transpose_k(0, half)
            keep_k(0, half)
        for tiles in (FIRST, SECOND):
            mask_on_scalar(0, tiles)
            mask_on_vector(0, tiles)
            for half in range(HALVES):
                scores(0, tiles.start, half)
                weigh(0, tiles.start, half)
            add_mask(0, tiles, cols=slice(0, S))
            if tiles == FIRST:
                transpose_q(0, slice(DUO, 2 * DUO))
                keep_q(0, slice(DUO, 2 * DUO))
            else:
                mask_on_scalar(1, BOTH)

        for r in range(DUOS):
            prepare_heads("load", r)
            for t in range(DUO):
                for half in range(HALVES):
                    if r > 0:
                        weigh(r, t, half)
                    run(scores, r + 1, t, half)
            if r == 0:
                for tiles in (slice(2 * DUO, SHRUNK_BY_MATMUL), slice(SHRUNK_BY_MATMUL, Q_TILES)):
                    transpose_q(0, tiles)
                    keep_q(0, tiles)
            prepare_heads("tensor", r)
            run(row_max, r - 2, BOTH)
            run(negate_max, r - 2, BOTH)
            run(exponent, r - 2, 0)
            run(exponent, r - 2, 1)
            prepare_heads("keep", r)
            prepare_heads("scalar", r)
            run(transpose_p, r - 2, 0)
            prepare_heads("vector", r)
            if r > 0:
                mask_on_vector(r, BOTH)
            run(quantise_p, r - 3, BOTH)
            if r > 0:
                add_mask(r, BOTH, nc.vector, slice(S - VECTOR_COLS, S))
            run(invert_sum, r - 3)
            run(weighted_sum, r - 3, 0, psum_o, "acc")
            run(weighted_sum, r - 3, 1, psum_o, "acc")
            run(transpose_p, r - 2, 1)
            run(normalise, r - 3, 0)
            run(normalise, r - 3, 1)
            run(store, r - 3, BOTH)
            if r < LAST:
                run(regroup_p, r - 2, 0, nc.scalar.copy)
                run(regroup_p, r - 2, 1, nc.scalar.copy)
            if r > 0:
                run(mask_on_scalar, r + 1, BOTH)
            for tiles in () if r == 0 else (FIRST, SECOND) if r == LAST else (BOTH,):
                add_mask(r, tiles)

        row_max(LAST - 1, BOTH)
        row_max(LAST, FIRST)
        for t in range(DUO):
            regroup_p(LAST - 2, t, nc.vector.tensor_copy)
        row_max(LAST, SECOND)
        quantise_p(LAST - 2, BOTH)
        invert_sum(LAST - 2)
        negate_max(LAST - 1, BOTH)
        exponent(LAST - 1, 0)
        transpose_p(LAST - 1, 0)
        exponent(LAST - 1, 1)
        transpose_p(LAST - 1, 1)
        for t in range(DUO):
            weighted_sum(LAST - 2, t, psum_o, "acc")
        for t in range(DUO):
            regroup_p(LAST - 1, t, nc.vector.tensor_copy)
        quantise_p(LAST - 1, BOTH)
        invert_sum(LAST - 1)
        negate_max(LAST, FIRST)
        exponent(LAST, 0)
        transpose_p(LAST, 0)
        negate_max(LAST, SECOND)
        exponent(LAST, 1)
        transpose_p(LAST, 1)
        normalise(LAST - 2, 0)
        normalise(LAST - 2, 1)
        store(LAST - 2, BOTH)
        regroup_p(LAST, 0, nc.vector.tensor_copy)
        quantise_p(LAST, FIRST)
        regroup_p(LAST, 1, nc.vector.tensor_copy)
        quantise_p(LAST, SECOND)
        invert_sum(LAST)
        for t in range(DUO):
            weighted_sum(LAST - 1, t, psum_sc, "sc")
        normalise(LAST - 1, 0)
        normalise(LAST - 1, 1)
        store(LAST - 1, BOTH)
        for t in range(DUO):
            weighted_sum(LAST, t, psum_sc, "sc")
        normalise(LAST, 0)
        store(LAST, FIRST)
        normalise(LAST, 1)
        store(LAST, SECOND)
